import numpy as np
import ml_dtypes


def mxq(x, axis, fmt="e4m3"):
    dtype, down = {"e4m3": (ml_dtypes.float8_e4m3fn, 7), "e5m2": (ml_dtypes.float8_e5m2, 14)}[fmt]
    v = np.moveaxis(np.asarray(x, np.float32).astype(ml_dtypes.bfloat16).astype(np.float64), axis, -1)
    blocks = v.reshape(v.shape[:-1] + (-1, 32))
    amax = np.abs(blocks).max(-1, keepdims=True)
    byte = np.maximum(np.where(amax > 0, np.frexp(amax)[1] - 1 + 127, 0) - down, 1)
    scale = np.exp2(byte - 127.0)
    codes = (blocks / scale).astype(np.float32).astype(dtype).astype(np.float64)
    return np.moveaxis((codes * scale).reshape(v.shape), -1, axis)


WIDE = False


def mx_kscale(k):
    if not WIDE:
        return np.ones(k)
    levels = np.array([10, -10, 5, -5, 0])
    a = np.random.permutation(np.resize(levels, k // 512 * 4)).reshape(k // 512, 4)
    idx = np.arange(k)
    return np.exp2(a[idx // 512, idx % 128 // 32])


BF16 = ml_dtypes.bfloat16


def bf(x):
    return np.asarray(x, np.float32).astype(BF16)


def f64(x):
    return np.asarray(x).astype(np.float64)


N, F, K, D, E = 512, 2048, 1536, 1024, 1024
QS = 2.0
PS = 16.0


def setup_inputs():
    s, t = mx_kscale(F), mx_kscale(E)
    return {"x": bf(np.random.standard_normal((N, F)) * s),
            "Wy_w": bf(np.random.standard_normal((E, F)) * QS * F ** -0.5 / s[None, :] * t[:, None]),
            "Wy_b": bf(np.random.standard_normal(E) * 0.2 * t),
            "k": bf(np.random.standard_normal((K, E)) / t[None, :]),
            "prior": bf(np.random.uniform(size=K) * PS)}


def reference(x, Wy_w, Wy_b, k, prior):
    scale = 1.0 / (E ** 0.5)
    q = (mxq(f64(x), 1, "e4m3") @ mxq(f64(Wy_w), 1, "e4m3").T) + f64(Wy_b)
    sc = (mxq(q, 1, "e4m3") @ mxq(f64(k), 1, "e4m3").T) * scale
    e = np.exp(sc - sc.max(-1, keepdims=True))
    att = e / e.sum(-1, keepdims=True)
    return att * f64(prior)[None, :]

@@ -1,0 +1,254 @@
+from contextlib import ExitStack
+
+import concourse.masks as masks
+import concourse.mybir as mybir
+
+F32 = mybir.dt.float32
+BF16 = mybir.dt.bfloat16
+U32 = mybir.dt.uint32
+U8 = mybir.dt.uint8
+FP8X4 = mybir.dt.float8_e4m3fn_x4
+ALU = mybir.AluOpType
+ACT = mybir.ActivationFunctionType
+AXIS = mybir.AxisListType
+
+P = 128
+BANK = 512
+N_ROWS, F_DIM, E_DIM, K_DICT = 512, 2048, 1024, 1536
+N_BLOCKS = N_ROWS // P
+F_PASSES = F_DIM // 512
+E_PASSES = E_DIM // 512
+J_CHUNKS = K_DICT // BANK
+UNIT = 4096
+SCALE = 1.0 / (E_DIM**0.5)
+
+FLOPS = 2 * N_ROWS * F_DIM * E_DIM + 2 * N_ROWS * E_DIM * K_DICT
+
+
+def tile_visualdeconfounder_pa_kernel(tc, x, Wy_w, Wy_b, k, prior, out):
+    nc = tc.nc
+    with ExitStack() as ctx:
+        ctx.enter_context(tc.manual_schedule())
+        const = ctx.enter_context(tc.tile_pool(name="const", bufs=1))
+        raw_pool = ctx.enter_context(tc.tile_pool(name="raw", bufs=1))
+        keep = ctx.enter_context(tc.tile_pool(name="keep", bufs=1))
+        grouped_pool = ctx.enter_context(tc.tile_pool(name="grouped", bufs=3))
+        soft = ctx.enter_context(tc.tile_pool(name="soft", bufs=2))
+        small = ctx.enter_context(tc.tile_pool(name="small", bufs=2))
+
+        x_raw = [raw_pool.tile([P, UNIT], BF16, name="x_raw%d" % a) for a in range(2)]
+        w_raw = [raw_pool.tile([P, UNIT], BF16, name="w_raw%d" % c) for c in range(4)]
+        k_raw = [raw_pool.tile([P, UNIT], BF16, name="k_raw%d" % c) for c in range(J_CHUNKS)]
+        for i in range(N_BLOCKS):
+            half = slice(F_DIM * (i % 2), F_DIM * (i % 2 + 1))
+            nc.sync.dma_start(out=x_raw[i // 2][:, half], in_=x[P * i : P * (i + 1), :])
+        for c in range(4):
+            rows = Wy_w[256 * c : 256 * (c + 1), :]
+            nc.sync.dma_start(out=w_raw[c][:], in_=rows.rearrange("(p s) f -> p (s f)", s=2))
+        for c in range(J_CHUNKS):
+            rows = k[BANK * c : BANK * (c + 1), :]
+            nc.sync.dma_start(
+                out=k_raw[c][:].rearrange("p (b e) -> p b e", b=4),
+                in_=rows.rearrange("(b p) e -> p b e", p=P),
+            )
+        prior_all = const.tile([P, K_DICT], BF16)
+        nc.sync.dma_start(out=prior_all[:], in_=prior.partition_broadcast(P))
+
+        zero = const.tile([P, 1], F32)
+        one = const.tile([P, 1], F32)
+        nc.vector.memset(zero[:], 0.0)
+        nc.scalar.activation(out=one[:], in_=zero[:], func=ACT.Exp)
+
+        ident = const.tile([P, P], F32)
+        masks.make_identity(nc, ident[:])
+
+        bias_bf = const.tile([P, 8], BF16)
+        with nc.allow_non_contiguous_dma(reason="1,024 bias values, two to a piece"):
+            nc.gpsimd.dma_start(
+                out=bias_bf[:].rearrange("p (c s) -> p c s", s=2),
+                in_=Wy_b.rearrange("(c p s) -> p c s", p=P, s=2),
+            )
+        bias = const.tile([P, 8], F32)
+        nc.vector.tensor_copy(out=bias[:], in_=bias_bf[:])
+
+        x_codes = keep.tile([P, N_BLOCKS * F_PASSES * P], U32, align_bytes=64)
+        x_scales = keep.tile([P, N_BLOCKS * F_PASSES * P], U8, align_bytes=64)
+        w_codes = keep.tile([P, 8 * F_PASSES * P], U32, align_bytes=64)
+        w_scales = keep.tile([P, 8 * F_PASSES * P], U8, align_bytes=64)
+        k_codes = keep.tile([P, E_PASSES * K_DICT], U32, align_bytes=64)
+        k_scales = keep.tile([P, E_PASSES * K_DICT], U8, align_bytes=64)
+        q_codes = keep.tile([P, E_PASSES * N_ROWS], U32, align_bytes=64)
+        q_scales = keep.tile([P, E_PASSES * N_ROWS], U8, align_bytes=64)
+        q_grouped = [
+            keep.tile([P, N_ROWS * 4], BF16, name="q_grouped%d" % g, align_bytes=64)
+            for g in range(E_PASSES)
+        ]
+
+        def quantise(grouped, codes, scales, first, width):
+            nc.vector.quantize_mx(
+                out=codes[:, first : first + width].bitcast(FP8X4),
+                scales=scales[:, first : first + width],
+                in_=grouped,
+            )
+
+        def mx_pass(acc, a_codes, a_scales, a_first, b_codes, b_scales, b_first, width, g, passes):
+            nc.tensor.matmul_mx(
+                out=acc,
+                lhsT=a_codes[:, a_first : a_first + P].bitcast(FP8X4),
+                lhsT_scale=a_scales[:, a_first : a_first + P],
+                rhs=b_codes[:, b_first : b_first + width].bitcast(FP8X4),
+                rhs_scale=b_scales[:, b_first : b_first + width],
+                start=(g == 0),
+                stop=(g == passes - 1),
+            )
+
+        with tc.psum_pool(name="q_psum", bufs=N_BLOCKS) as q_psum, tc.psum_pool(
+            name="t_psum", bufs=4
+        ) as t_psum:
+
+            def transpose_unit(raw, k_order):
+                words = raw[:].bitcast(F32)
+                grouped = grouped_pool.tile([P, UNIT], BF16, align_bytes=64)
+                if k_order:
+                    dest = grouped[:].bitcast(F32).rearrange("p (g b r u) -> p b g r u", g=2, b=4, u=2)
+                else:
+                    dest = grouped[:].bitcast(F32).rearrange("p (b g r u) -> p b g r u", g=2, b=4, u=2)
+                for b in range(4):
+                    bank = t_psum.tile([P, 4, P], F32)
+                    for v in range(4):
+                        first = BANK * b + P * v
+                        nc.tensor.transpose(bank[:, v, :], words[:, first : first + P], ident[:])
+                    nc.scalar.copy(
+                        out=dest[:, b], in_=bank[:].rearrange("p (g u) r -> p g r u", u=2)
+                    )
+                return grouped
+
+            def first_product(c, q_banks):
+                for s in range(2):
+                    t = 2 * (c % 2) + s
+                    for i in range(N_BLOCKS):
+                        for g in range(F_PASSES):
+                            mx_pass(
+                                q_banks[i][:, t, :],
+                                w_codes, w_scales, ((2 * c + s) * F_PASSES + g) * P,
+                                x_codes, x_scales, (i * F_PASSES + g) * P,
+                                P, g, F_PASSES,
+                            )
+
+            def finish_q(g, q_banks):
+                bias_tn = bias[:, 4 * g : 4 * g + 4].unsqueeze(1).to_broadcast([P, P, 4])
+                for i in range(N_BLOCKS + 1):
+                    if i < N_BLOCKS:
+                        nc.vector.tensor_tensor(
+                            out=q_grouped[g][:, BANK * i : BANK * (i + 1)].rearrange(
+                                "p (n t) -> p n t", t=4
+                            ),
+                            in0=q_banks[i][:].rearrange("p t n -> p n t"),
+                            in1=bias_tn,
+                            op=ALU.add,
+                        )
+                    if i > 0:
+                        quantise(
+                            q_grouped[g][:, BANK * (i - 1) : BANK * i],
+                            q_codes, q_scales, g * N_ROWS + P * (i - 1), P,
+                        )
+
+            def prepare(raw, k_order, codes, scales, first_of_half):
+                grouped = transpose_unit(raw, k_order)
+                for h in range(2):
+                    quantise(
+                        grouped[:, 2048 * h : 2048 * (h + 1)], codes, scales, first_of_half[h], BANK
+                    )
+
+            def prepare_k(c):
+                prepare(k_raw[c], True, k_codes, k_scales, [BANK * c, K_DICT + BANK * c])
+
+            for a in range(2):
+                prepare(x_raw[a], False, x_codes, x_scales, [2 * a * BANK, (2 * a + 1) * BANK])
+            prepare(w_raw[0], False, w_codes, w_scales, [0, BANK])
+            q_banks = []
+            for c in range(4):
+                if c + 1 < 4:
+                    first = 2 * (c + 1) * BANK
+                    prepare(w_raw[c + 1], False, w_codes, w_scales, [first, first + BANK])
+                else:
+                    prepare_k(0)
+                if c % 2 == 0:
+                    q_banks = [
+                        q_psum.tile([P, 4, P], F32, name="q_bank%d" % i, tag="q_bank")
+                        for i in range(N_BLOCKS)
+                    ]
+                first_product(c, q_banks)
+                if c % 2 == 1:
+                    finish_q(c // 2, q_banks)
+            prepare_k(1)
+            prepare_k(2)
+
+        with tc.psum_pool(name="s_psum", bufs=8, reuse_waits="tile") as s_psum:
+
+            def scores(i):
+                banks = []
+                for c in range(J_CHUNKS):
+                    bank = s_psum.tile([P, BANK], F32, name="s_bank")
+                    for g in range(E_PASSES):
+                        mx_pass(
+                            bank[:],
+                            q_codes, q_scales, g * N_ROWS + P * i,
+                            k_codes, k_scales, g * K_DICT + BANK * c,
+                            BANK, g, E_PASSES,
+                        )
+                    banks.append(bank)
+                return banks
+
+            def row_maximum(banks):
+                chunk_max = small.tile([P, J_CHUNKS], F32)
+                for c in range(J_CHUNKS):
+                    nc.vector.tensor_reduce(
+                        out=chunk_max[:, c : c + 1], in_=banks[c][:], axis=AXIS.X, op=ALU.max
+                    )
+                row_max = small.tile([P, 1], F32)
+                nc.vector.tensor_reduce(out=row_max[:], in_=chunk_max[:], axis=AXIS.X, op=ALU.max)
+                shift = small.tile([P, 1], F32)
+                nc.vector.tensor_scalar_mul(shift[:], row_max[:], -SCALE)
+                return shift
+
+            def exponentials(banks, shift):
+                e = soft.tile([P, K_DICT], F32)
+                chunk_sum = small.tile([P, J_CHUNKS], F32)
+                for c in range(J_CHUNKS):
+                    nc.scalar.activation(
+                        out=e[:, BANK * c : BANK * (c + 1)],
+                        in_=banks[c][:],
+                        func=ACT.Exp,
+                        bias=shift[:],
+                        scale=SCALE,
+                        accum_out=chunk_sum[:, c : c + 1],
+                    )
+                return e, chunk_sum
+
+            def normalise_and_store(i, e, chunk_sum):
+                row_sum = small.tile([P, 1], F32)
+                nc.vector.tensor_reduce(out=row_sum[:], in_=chunk_sum[:], axis=AXIS.X, op=ALU.add)
+                inverse = small.tile([P, 1], F32)
+                nc.vector.reciprocal(inverse[:], row_sum[:])
+                result = soft.tile([P, K_DICT], F32)
+                for c in range(J_CHUNKS):
+                    cols = slice(BANK * c, BANK * (c + 1))
+                    nc.vector.scalar_tensor_tensor(
+                        out=result[:, cols],
+                        in0=e[:, cols],
+                        scalar=inverse[:],
+                        in1=prior_all[:, cols],
+                        op0=ALU.mult,
+                        op1=ALU.mult,
+                    )
+                    nc.sync.dma_start(out=out[P * i : P * (i + 1), cols], in_=result[:, cols])
+
+            banks = scores(0)
+            shift = row_maximum(banks)
+            for i in range(N_BLOCKS):
+                e, chunk_sum = exponentials(banks, shift)
+                if i + 1 < N_BLOCKS:
+                    banks = scores(i + 1)
+                    shift = row_maximum(banks)
+                normalise_and_store(i, e, chunk_sum)

@@ -39,18 +39,24 @@ def tile_visualdeconfounder_pa_kernel(tc, x, Wy_w, Wy_b, k, prior, out):
         x_raw = [raw_pool.tile([P, UNIT], BF16, name="x_raw%d" % a) for a in range(2)]
         w_raw = [raw_pool.tile([P, UNIT], BF16, name="w_raw%d" % c) for c in range(4)]
         k_raw = [raw_pool.tile([P, UNIT], BF16, name="k_raw%d" % c) for c in range(J_CHUNKS)]
-        for i in range(N_BLOCKS):
-            half = slice(F_DIM * (i % 2), F_DIM * (i % 2 + 1))
-            nc.sync.dma_start(out=x_raw[i // 2][:, half], in_=x[P * i : P * (i + 1), :])
-        for c in range(4):
+        def load_w(c):
             rows = Wy_w[256 * c : 256 * (c + 1), :]
             nc.sync.dma_start(out=w_raw[c][:], in_=rows.rearrange("(p s) f -> p (s f)", s=2))
-        for c in range(J_CHUNKS):
+
+        def load_k(c):
             rows = k[BANK * c : BANK * (c + 1), :]
             nc.sync.dma_start(
                 out=k_raw[c][:].rearrange("p (b e) -> p b e", b=4),
                 in_=rows.rearrange("(b p) e -> p b e", p=P),
             )
+
+        for i in range(N_BLOCKS):
+            half = slice(F_DIM * (i % 2), F_DIM * (i % 2 + 1))
+            nc.sync.dma_start(out=x_raw[i // 2][:, half], in_=x[P * i : P * (i + 1), :])
+        load_w(0)
+        for c in range(J_CHUNKS):
+            load_w(c + 1)
+            load_k(c)
         prior_all = const.tile([P, K_DICT], BF16)
         nc.sync.dma_start(out=prior_all[:], in_=prior.partition_broadcast(P))
 
@@ -64,12 +70,11 @@ def tile_visualdeconfounder_pa_kernel(tc, x, Wy_w, Wy_b, k, prior, out):
 
         bias_bf = const.tile([P, 8], BF16)
         with nc.allow_non_contiguous_dma(reason="1,024 bias values, two to a piece"):
-            nc.gpsimd.dma_start(
+            nc.scalar.dma_start(
                 out=bias_bf[:].rearrange("p (c s) -> p c s", s=2),
                 in_=Wy_b.rearrange("(c p s) -> p c s", p=P, s=2),
             )
         bias = const.tile([P, 8], F32)
-        nc.vector.tensor_copy(out=bias[:], in_=bias_bf[:])
 
         x_codes = keep.tile([P, N_BLOCKS * F_PASSES * P], U32, align_bytes=64)
         x_scales = keep.tile([P, N_BLOCKS * F_PASSES * P], U8, align_bytes=64)
@@ -124,9 +129,9 @@ def tile_visualdeconfounder_pa_kernel(tc, x, Wy_w, Wy_b, k, prior, out):
                 return grouped
 
             def first_product(c, q_banks):
-                for s in range(2):
-                    t = 2 * (c % 2) + s
-                    for i in range(N_BLOCKS):
+                for i in range(N_BLOCKS):
+                    for s in range(2):
+                        t = 2 * (c % 2) + s
                         for g in range(F_PASSES):
                             mx_pass(
                                 q_banks[i][:, t, :],
@@ -163,16 +168,19 @@ def tile_visualdeconfounder_pa_kernel(tc, x, Wy_w, Wy_b, k, prior, out):
             def prepare_k(c):
                 prepare(k_raw[c], True, k_codes, k_scales, [BANK * c, K_DICT + BANK * c])
 
+            def prepare_w(c):
+                prepare(w_raw[c], False, w_codes, w_scales, [2 * c * BANK, (2 * c + 1) * BANK])
+
             for a in range(2):
                 prepare(x_raw[a], False, x_codes, x_scales, [2 * a * BANK, (2 * a + 1) * BANK])
-            prepare(w_raw[0], False, w_codes, w_scales, [0, BANK])
+            prepare_w(0)
+            nc.vector.tensor_copy(out=bias[:], in_=bias_bf[:])
             q_banks = []
             for c in range(4):
+                if c > 0:
+                    prepare_k(c - 1)
                 if c + 1 < 4:
-                    first = 2 * (c + 1) * BANK
-                    prepare(w_raw[c + 1], False, w_codes, w_scales, [first, first + BANK])
-                else:
-                    prepare_k(0)
+                    prepare_w(c + 1)
                 if c % 2 == 0:
                     q_banks = [
                         q_psum.tile([P, 4, P], F32, name="q_bank%d" % i, tag="q_bank")
@@ -181,8 +189,6 @@ def tile_visualdeconfounder_pa_kernel(tc, x, Wy_w, Wy_b, k, prior, out):
                 first_product(c, q_banks)
                 if c % 2 == 1:
                     finish_q(c // 2, q_banks)
-            prepare_k(1)
-            prepare_k(2)
 
         with tc.psum_pool(name="s_psum", bufs=8, reuse_waits="tile") as s_psum:
 

@@ -54,9 +54,12 @@ def tile_visualdeconfounder_pa_kernel(tc, x, Wy_w, Wy_b, k, prior, out):
             half = slice(F_DIM * (i % 2), F_DIM * (i % 2 + 1))
             nc.sync.dma_start(out=x_raw[i // 2][:, half], in_=x[P * i : P * (i + 1), :])
         load_w(0)
-        for c in range(J_CHUNKS):
-            load_w(c + 1)
-            load_k(c)
+        load_w(1)
+        load_w(2)
+        load_k(0)
+        load_w(3)
+        load_k(1)
+        load_k(2)
         prior_all = const.tile([P, K_DICT], BF16)
         nc.sync.dma_start(out=prior_all[:], in_=prior.partition_broadcast(P))
 
@@ -128,17 +131,16 @@ def tile_visualdeconfounder_pa_kernel(tc, x, Wy_w, Wy_b, k, prior, out):
                     )
                 return grouped
 
-            def first_product(c, q_banks):
+            def first_product(c, s, q_banks):
+                t = 2 * (c % 2) + s
                 for i in range(N_BLOCKS):
-                    for s in range(2):
-                        t = 2 * (c % 2) + s
-                        for g in range(F_PASSES):
-                            mx_pass(
-                                q_banks[i][:, t, :],
-                                w_codes, w_scales, ((2 * c + s) * F_PASSES + g) * P,
-                                x_codes, x_scales, (i * F_PASSES + g) * P,
-                                P, g, F_PASSES,
-                            )
+                    for g in range(F_PASSES):
+                        mx_pass(
+                            q_banks[i][:, t, :],
+                            w_codes, w_scales, ((2 * c + s) * F_PASSES + g) * P,
+                            x_codes, x_scales, (i * F_PASSES + g) * P,
+                            P, g, F_PASSES,
+                        )
 
             def finish_q(g, q_banks):
                 bias_tn = bias[:, 4 * g : 4 * g + 4].unsqueeze(1).to_broadcast([P, P, 4])
@@ -165,30 +167,37 @@ def tile_visualdeconfounder_pa_kernel(tc, x, Wy_w, Wy_b, k, prior, out):
                         grouped[:, 2048 * h : 2048 * (h + 1)], codes, scales, first_of_half[h], BANK
                     )
 
-            def prepare_k(c):
-                prepare(k_raw[c], True, k_codes, k_scales, [BANK * c, K_DICT + BANK * c])
+            def prepare_x(a):
+                prepare(x_raw[a], False, x_codes, x_scales, [2 * a * BANK, (2 * a + 1) * BANK])
 
             def prepare_w(c):
                 prepare(w_raw[c], False, w_codes, w_scales, [2 * c * BANK, (2 * c + 1) * BANK])
 
-            for a in range(2):
-                prepare(x_raw[a], False, x_codes, x_scales, [2 * a * BANK, (2 * a + 1) * BANK])
+            def prepare_k(c):
+                prepare(k_raw[c], True, k_codes, k_scales, [BANK * c, K_DICT + BANK * c])
+
+            prepare_x(0)
+            prepare_x(1)
             prepare_w(0)
             nc.vector.tensor_copy(out=bias[:], in_=bias_bf[:])
+            later_units = [
+                (prepare_w, 1), (prepare_w, 2), (prepare_k, 0),
+                (prepare_w, 3), (prepare_k, 1), (prepare_k, 2),
+            ]
             q_banks = []
-            for c in range(4):
-                if c > 0:
-                    prepare_k(c - 1)
-                if c + 1 < 4:
-                    prepare_w(c + 1)
-                if c % 2 == 0:
+            for group in range(8):
+                c, s = divmod(group, 2)
+                if group % 4 == 0:
                     q_banks = [
                         q_psum.tile([P, 4, P], F32, name="q_bank%d" % i, tag="q_bank")
                         for i in range(N_BLOCKS)
                     ]
-                first_product(c, q_banks)
-                if c % 2 == 1:
-                    finish_q(c // 2, q_banks)
+                first_product(c, s, q_banks)
+                if group % 4 == 3:
+                    finish_q(group // 4, q_banks)
+                if group < len(later_units):
+                    prepare_unit, index = later_units[group]
+                    prepare_unit(index)
 
         with tc.psum_pool(name="s_psum", bufs=8, reuse_waits="tile") as s_psum:
 

@@ -33,7 +33,7 @@ def tile_visualdeconfounder_pa_kernel(tc, x, Wy_w, Wy_b, k, prior, out):
         raw_pool = ctx.enter_context(tc.tile_pool(name="raw", bufs=1))
         keep = ctx.enter_context(tc.tile_pool(name="keep", bufs=1))
         grouped_pool = ctx.enter_context(tc.tile_pool(name="grouped", bufs=3))
-        soft = ctx.enter_context(tc.tile_pool(name="soft", bufs=2))
+        soft = ctx.enter_context(tc.tile_pool(name="soft", bufs=3))
         small = ctx.enter_context(tc.tile_pool(name="small", bufs=2))
 
         x_raw = [raw_pool.tile([P, UNIT], BF16, name="x_raw%d" % a) for a in range(2)]
@@ -55,6 +55,12 @@ def tile_visualdeconfounder_pa_kernel(tc, x, Wy_w, Wy_b, k, prior, out):
             nc.sync.dma_start(out=x_raw[i // 2][:, half], in_=x[P * i : P * (i + 1), :])
         load_w(0)
         load_w(1)
+        bias_bf = const.tile([P, 8], BF16)
+        with nc.allow_non_contiguous_dma(reason="1,024 bias values, two to a piece"):
+            nc.sync.dma_start(
+                out=bias_bf[:].rearrange("p (c s) -> p c s", s=2),
+                in_=Wy_b.rearrange("(c p s) -> p c s", p=P, s=2),
+            )
         load_w(2)
         load_k(0)
         load_w(3)
@@ -71,12 +77,6 @@ def tile_visualdeconfounder_pa_kernel(tc, x, Wy_w, Wy_b, k, prior, out):
         ident = const.tile([P, P], F32)
         masks.make_identity(nc, ident[:])
 
-        bias_bf = const.tile([P, 8], BF16)
-        with nc.allow_non_contiguous_dma(reason="1,024 bias values, two to a piece"):
-            nc.scalar.dma_start(
-                out=bias_bf[:].rearrange("p (c s) -> p c s", s=2),
-                in_=Wy_b.rearrange("(c p s) -> p c s", p=P, s=2),
-            )
         bias = const.tile([P, 8], F32)
 
         x_codes = keep.tile([P, N_BLOCKS * F_PASSES * P], U32, align_bytes=64)
@@ -179,7 +179,6 @@ def tile_visualdeconfounder_pa_kernel(tc, x, Wy_w, Wy_b, k, prior, out):
             prepare_x(0)
             prepare_x(1)
             prepare_w(0)
-            nc.vector.tensor_copy(out=bias[:], in_=bias_bf[:])
             later_units = [
                 (prepare_w, 1), (prepare_w, 2), (prepare_k, 0),
                 (prepare_w, 3), (prepare_k, 1), (prepare_k, 2),
@@ -193,6 +192,8 @@ def tile_visualdeconfounder_pa_kernel(tc, x, Wy_w, Wy_b, k, prior, out):
                         for i in range(N_BLOCKS)
                     ]
                 first_product(c, s, q_banks)
+                if group == 0:
+                    nc.vector.tensor_copy(out=bias[:], in_=bias_bf[:])
                 if group % 4 == 3:
                     finish_q(group // 4, q_banks)
                 if group < len(later_units):
@@ -227,43 +228,53 @@ def tile_visualdeconfounder_pa_kernel(tc, x, Wy_w, Wy_b, k, prior, out):
                 nc.vector.tensor_scalar_mul(shift[:], row_max[:], -SCALE)
                 return shift
 
+            def maximum_of(i):
+                banks = scores(i)
+                return banks, row_maximum(banks)
+
             def exponentials(banks, shift):
                 e = soft.tile([P, K_DICT], F32)
+                result = soft.tile([P, K_DICT], F32)
                 chunk_sum = small.tile([P, J_CHUNKS], F32)
                 for c in range(J_CHUNKS):
+                    cols = slice(BANK * c, BANK * (c + 1))
                     nc.scalar.activation(
-                        out=e[:, BANK * c : BANK * (c + 1)],
+                        out=e[:, cols],
                         in_=banks[c][:],
                         func=ACT.Exp,
                         bias=shift[:],
                         scale=SCALE,
                         accum_out=chunk_sum[:, c : c + 1],
                     )
-                return e, chunk_sum
+                    if c < J_CHUNKS - 1:
+                        nc.gpsimd.tensor_tensor(
+                            out=result[:, cols], in0=e[:, cols], in1=prior_all[:, cols], op=ALU.mult
+                        )
+                return e, result, chunk_sum
 
-            def normalise_and_store(i, e, chunk_sum):
+            def normalise_and_store(i, e, result, chunk_sum):
+                rows = out[P * i : P * (i + 1), :]
+                first, last = slice(0, K_DICT - BANK), slice(K_DICT - BANK, K_DICT)
                 row_sum = small.tile([P, 1], F32)
                 nc.vector.tensor_reduce(out=row_sum[:], in_=chunk_sum[:], axis=AXIS.X, op=ALU.add)
                 inverse = small.tile([P, 1], F32)
                 nc.vector.reciprocal(inverse[:], row_sum[:])
-                result = soft.tile([P, K_DICT], F32)
-                for c in range(J_CHUNKS):
-                    cols = slice(BANK * c, BANK * (c + 1))
-                    nc.vector.scalar_tensor_tensor(
-                        out=result[:, cols],
-                        in0=e[:, cols],
-                        scalar=inverse[:],
-                        in1=prior_all[:, cols],
-                        op0=ALU.mult,
-                        op1=ALU.mult,
-                    )
-                    nc.sync.dma_start(out=out[P * i : P * (i + 1), cols], in_=result[:, cols])
+                nc.vector.scalar_tensor_tensor(
+                    out=result[:, last],
+                    in0=e[:, last],
+                    scalar=inverse[:],
+                    in1=prior_all[:, last],
+                    op0=ALU.mult,
+                    op1=ALU.mult,
+                )
+                nc.sync.dma_start(out=rows[:, last], in_=result[:, last])
+                nc.scalar.activation(
+                    out=result[:, first], in_=result[:, first], func=ACT.Copy, scale=inverse[:]
+                )
+                nc.sync.dma_start(out=rows[:, first], in_=result[:, first])
 
-            banks = scores(0)
-            shift = row_maximum(banks)
+            parts = exponentials(*maximum_of(0))
             for i in range(N_BLOCKS):
-                e, chunk_sum = exponentials(banks, shift)
-                if i + 1 < N_BLOCKS:
-                    banks = scores(i + 1)
-                    shift = row_maximum(banks)
-                normalise_and_store(i, e, chunk_sum)
+                next_parts = exponentials(*maximum_of(i + 1)) if i + 1 < N_BLOCKS else None
+                normalise_and_store(i, *parts)
+                parts = next_parts

@@ -50,9 +50,14 @@ def tile_visualdeconfounder_pa_kernel(tc, x, Wy_w, Wy_b, k, prior, out):
                 in_=rows.rearrange("(b p) e -> p b e", p=P),
             )
 
-        for i in range(N_BLOCKS):
-            half = slice(F_DIM * (i % 2), F_DIM * (i % 2 + 1))
-            nc.sync.dma_start(out=x_raw[i // 2][:, half], in_=x[P * i : P * (i + 1), :])
+        def load_x(a):
+            for b in range(2):
+                i = 2 * a + b
+                nc.sync.dma_start(
+                    out=x_raw[a][:, F_DIM * b : F_DIM * (b + 1)], in_=x[P * i : P * (i + 1), :]
+                )
+
+        load_x(0)
         load_w(0)
         load_w(1)
         bias_bf = const.tile([P, 8], BF16)
@@ -62,10 +67,11 @@ def tile_visualdeconfounder_pa_kernel(tc, x, Wy_w, Wy_b, k, prior, out):
                 in_=Wy_b.rearrange("(c p s) -> p c s", p=P, s=2),
             )
         load_w(2)
-        load_k(0)
         load_w(3)
+        load_k(0)
         load_k(1)
         load_k(2)
+        load_x(1)
         prior_all = const.tile([P, K_DICT], BF16)
         nc.sync.dma_start(out=prior_all[:], in_=prior.partition_broadcast(P))
 
@@ -110,17 +116,59 @@ def tile_visualdeconfounder_pa_kernel(tc, x, Wy_w, Wy_b, k, prior, out):
                 stop=(g == passes - 1),
             )
 
-        with tc.psum_pool(name="q_psum", bufs=N_BLOCKS) as q_psum, tc.psum_pool(
-            name="t_psum", bufs=4
-        ) as t_psum:
+        q_psum = ctx.enter_context(tc.psum_pool(name="q_psum", bufs=2))
 
-            def transpose_unit(raw, k_order):
-                words = raw[:].bitcast(F32)
+        def new_q_banks():
+            return [q_psum.tile([P, 4, P], F32, name="q_bank%d" % b, tag="q_bank") for b in range(2)]
+
+        def first_product(c, s, a, q_banks):
+            t = 2 * (c % 2) + s
+            for b in range(2):
+                for g in range(F_PASSES):
+                    mx_pass(
+                        q_banks[b][:, t, :],
+                        w_codes, w_scales, ((2 * c + s) * F_PASSES + g) * P,
+                        x_codes, x_scales, ((2 * a + b) * F_PASSES + g) * P,
+                        P, g, F_PASSES,
+                    )
+
+        def finish_q(g, a, q_banks):
+            bias_tn = bias[:, 4 * g : 4 * g + 4].unsqueeze(1).to_broadcast([P, P, 4])
+            for b in range(2):
+                i = 2 * a + b
+                nc.vector.tensor_tensor(
+                    out=q_grouped[g][:, BANK * i : BANK * (i + 1)].rearrange("p (n t) -> p n t", t=4),
+                    in0=q_banks[b][:].rearrange("p t n -> p n t"),
+                    in1=bias_tn,
+                    op=ALU.add,
+                )
+            for b in range(2):
+                i = 2 * a + b
+                quantise(
+                    q_grouped[g][:, BANK * i : BANK * (i + 1)], q_codes, q_scales, g * N_ROWS + P * i, P
+                )
+
+        x_units = [
+            (x_raw[a], False, x_codes, x_scales, [2 * a * BANK, (2 * a + 1) * BANK]) for a in range(2)
+        ]
+        w_units = [
+            (w_raw[c], False, w_codes, w_scales, [2 * c * BANK, (2 * c + 1) * BANK]) for c in range(4)
+        ]
+        k_units = [
+            (k_raw[c], True, k_codes, k_scales, [BANK * c, K_DICT + BANK * c]) for c in range(J_CHUNKS)
+        ]
+
+        def quantise_unit(unit, grouped):
+            for h in range(2):
+                quantise(grouped[:, 2048 * h : 2048 * (h + 1)], unit[2], unit[3], unit[4][h], BANK)
+
+        with tc.psum_pool(name="t_psum", bufs=6) as t_psum:
+
+            def transpose_unit(unit):
+                words = unit[0][:].bitcast(F32)
                 grouped = grouped_pool.tile([P, UNIT], BF16, align_bytes=64)
-                if k_order:
-                    dest = grouped[:].bitcast(F32).rearrange("p (g b r u) -> p b g r u", g=2, b=4, u=2)
-                else:
-                    dest = grouped[:].bitcast(F32).rearrange("p (b g r u) -> p b g r u", g=2, b=4, u=2)
+                order = "p (g b r u) -> p b g r u" if unit[1] else "p (b g r u) -> p b g r u"
+                dest = grouped[:].bitcast(F32).rearrange(order, g=2, b=4, u=2)
                 for b in range(4):
                     bank = t_psum.tile([P, 4, P], F32)
                     for v in range(4):
@@ -131,76 +179,25 @@ def tile_visualdeconfounder_pa_kernel(tc, x, Wy_w, Wy_b, k, prior, out):
                     )
                 return grouped
 
-            def first_product(c, s, q_banks):
-                t = 2 * (c % 2) + s
-                for i in range(N_BLOCKS):
-                    for g in range(F_PASSES):
-                        mx_pass(
-                            q_banks[i][:, t, :],
-                            w_codes, w_scales, ((2 * c + s) * F_PASSES + g) * P,
-                            x_codes, x_scales, (i * F_PASSES + g) * P,
-                            P, g, F_PASSES,
-                        )
-
-            def finish_q(g, q_banks):
-                bias_tn = bias[:, 4 * g : 4 * g + 4].unsqueeze(1).to_broadcast([P, P, 4])
-                for i in range(N_BLOCKS + 1):
-                    if i < N_BLOCKS:
-                        nc.vector.tensor_tensor(
-                            out=q_grouped[g][:, BANK * i : BANK * (i + 1)].rearrange(
-                                "p (n t) -> p n t", t=4
-                            ),
-                            in0=q_banks[i][:].rearrange("p t n -> p n t"),
-                            in1=bias_tn,
-                            op=ALU.add,
-                        )
-                    if i > 0:
-                        quantise(
-                            q_grouped[g][:, BANK * (i - 1) : BANK * i],
-                            q_codes, q_scales, g * N_ROWS + P * (i - 1), P,
-                        )
-
-            def prepare(raw, k_order, codes, scales, first_of_half):
-                grouped = transpose_unit(raw, k_order)
-                for h in range(2):
-                    quantise(
-                        grouped[:, 2048 * h : 2048 * (h + 1)], codes, scales, first_of_half[h], BANK
-                    )
-
-            def prepare_x(a):
-                prepare(x_raw[a], False, x_codes, x_scales, [2 * a * BANK, (2 * a + 1) * BANK])
-
-            def prepare_w(c):
-                prepare(w_raw[c], False, w_codes, w_scales, [2 * c * BANK, (2 * c + 1) * BANK])
-
-            def prepare_k(c):
-                prepare(k_raw[c], True, k_codes, k_scales, [BANK * c, K_DICT + BANK * c])
-
-            prepare_x(0)
-            prepare_x(1)
-            prepare_w(0)
-            later_units = [
-                (prepare_w, 1), (prepare_w, 2), (prepare_k, 0),
-                (prepare_w, 3), (prepare_k, 1), (prepare_k, 2),
-            ]
+            for unit in [x_units[0], w_units[0]]:
+                quantise_unit(unit, transpose_unit(unit))
+            later_units = w_units[1:] + k_units
             q_banks = []
             for group in range(8):
                 c, s = divmod(group, 2)
+                grouped = transpose_unit(later_units[group]) if group < len(later_units) else None
                 if group % 4 == 0:
-                    q_banks = [
-                        q_psum.tile([P, 4, P], F32, name="q_bank%d" % i, tag="q_bank")
-                        for i in range(N_BLOCKS)
-                    ]
-                first_product(c, s, q_banks)
+                    q_banks = new_q_banks()
+                first_product(c, s, 0, q_banks)
                 if group == 0:
                     nc.vector.tensor_copy(out=bias[:], in_=bias_bf[:])
                 if group % 4 == 3:
-                    finish_q(group // 4, q_banks)
+                    finish_q(group // 4, 0, q_banks)
                 if group < len(later_units):
-                    prepare_unit, index = later_units[group]
-                    prepare_unit(index)
+                    quantise_unit(later_units[group], grouped)
+            quantise_unit(x_units[1], transpose_unit(x_units[1]))
 
-        with tc.psum_pool(name="s_psum", bufs=8, reuse_waits="tile") as s_psum:
+        with tc.psum_pool(name="s_psum", bufs=6, reuse_waits="tile") as s_psum:
 
             def scores(i):
                 banks = []
@@ -273,8 +270,17 @@ def tile_visualdeconfounder_pa_kernel(tc, x, Wy_w, Wy_b, k, prior, out):
                 )
                 nc.sync.dma_start(out=rows[:, first], in_=result[:, first])
 
-            parts = exponentials(*maximum_of(0))
-            for i in range(N_BLOCKS):
-                next_parts = exponentials(*maximum_of(i + 1)) if i + 1 < N_BLOCKS else None
-                normalise_and_store(i, *parts)
-                parts = next_parts
+            started = [exponentials(*maximum_of(i)) for i in range(2)]
+            q_banks = new_q_banks()
+            for t in range(4):
+                first_product(t // 2, t % 2, 1, q_banks)
+            finish_q(0, 1, q_banks)
+            normalise_and_store(0, *started[0])
+            q_banks = new_q_banks()
+            for t in range(4):
+                first_product(2 + t // 2, t % 2, 1, q_banks)
+            normalise_and_store(1, *started[1])
+            finish_q(1, 1, q_banks)
+            started = [exponentials(*maximum_of(i)) for i in range(2, 4)]
+            normalise_and_store(2, *started[0])
+            normalise_and_store(3, *started[1])

@@ -174,9 +174,11 @@ def tile_visualdeconfounder_pa_kernel(tc, x, Wy_w, Wy_b, k, prior, out):
                     for v in range(4):
                         first = BANK * b + P * v
                         nc.tensor.transpose(bank[:, v, :], words[:, first : first + P], ident[:])
-                    nc.scalar.copy(
-                        out=dest[:, b], in_=bank[:].rearrange("p (g u) r -> p g r u", u=2)
-                    )
+                    planes = bank[:].rearrange("p (g u) r -> p g r u", u=2)
+                    if b == 0:
+                        nc.vector.tensor_copy(out=dest[:, b], in_=planes)
+                    else:
+                        nc.scalar.copy(out=dest[:, b], in_=planes)
                 return grouped
 
             for unit in [x_units[0], w_units[0]]:

from contextlib import ExitStack

import concourse.masks as masks
import concourse.mybir as mybir

F32 = mybir.dt.float32
BF16 = mybir.dt.bfloat16
U32 = mybir.dt.uint32
U8 = mybir.dt.uint8
FP8X4 = mybir.dt.float8_e4m3fn_x4
ALU = mybir.AluOpType
ACT = mybir.ActivationFunctionType
AXIS = mybir.AxisListType

P = 128
BANK = 512
N_ROWS, F_DIM, E_DIM, K_DICT = 512, 2048, 1024, 1536
N_BLOCKS = N_ROWS // P
F_PASSES = F_DIM // 512
E_PASSES = E_DIM // 512
J_CHUNKS = K_DICT // BANK
UNIT = 4096
SCALE = 1.0 / (E_DIM**0.5)

FLOPS = 2 * N_ROWS * F_DIM * E_DIM + 2 * N_ROWS * E_DIM * K_DICT


def tile_visualdeconfounder_pa_kernel(tc, x, Wy_w, Wy_b, k, prior, out):
    nc = tc.nc
    with ExitStack() as ctx:
        ctx.enter_context(tc.manual_schedule())
        const = ctx.enter_context(tc.tile_pool(name="const", bufs=1))
        raw_pool = ctx.enter_context(tc.tile_pool(name="raw", bufs=1))
        keep = ctx.enter_context(tc.tile_pool(name="keep", bufs=1))
        grouped_pool = ctx.enter_context(tc.tile_pool(name="grouped", bufs=3))
        soft = ctx.enter_context(tc.tile_pool(name="soft", bufs=3))
        small = ctx.enter_context(tc.tile_pool(name="small", bufs=2))

        x_raw = [raw_pool.tile([P, UNIT], BF16, name="x_raw%d" % a) for a in range(2)]
        w_raw = [raw_pool.tile([P, UNIT], BF16, name="w_raw%d" % c) for c in range(4)]
        k_raw = [raw_pool.tile([P, UNIT], BF16, name="k_raw%d" % c) for c in range(J_CHUNKS)]
        def load_w(c):
            rows = Wy_w[256 * c : 256 * (c + 1), :]
            nc.sync.dma_start(out=w_raw[c][:], in_=rows.rearrange("(p s) f -> p (s f)", s=2))

        def load_k(c):
            rows = k[BANK * c : BANK * (c + 1), :]
            nc.sync.dma_start(
                out=k_raw[c][:].rearrange("p (b e) -> p b e", b=4),
                in_=rows.rearrange("(b p) e -> p b e", p=P),
            )

        def load_x(a):
            for b in range(2):
                i = 2 * a + b
                nc.sync.dma_start(
                    out=x_raw[a][:, F_DIM * b : F_DIM * (b + 1)], in_=x[P * i : P * (i + 1), :]
                )

        load_x(0)
        load_w(0)
        load_w(1)
        bias_bf = const.tile([P, 8], BF16)
        with nc.allow_non_contiguous_dma(reason="1,024 bias values, two to a piece"):
            nc.sync.dma_start(
                out=bias_bf[:].rearrange("p (c s) -> p c s", s=2),
                in_=Wy_b.rearrange("(c p s) -> p c s", p=P, s=2),
            )
        load_w(2)
        load_w(3)
        load_k(0)
        load_k(1)
        load_k(2)
        load_x(1)
        prior_all = const.tile([P, K_DICT], BF16)
        nc.sync.dma_start(out=prior_all[:], in_=prior.partition_broadcast(P))

        zero = const.tile([P, 1], F32)
        one = const.tile([P, 1], F32)
        nc.vector.memset(zero[:], 0.0)
        nc.scalar.activation(out=one[:], in_=zero[:], func=ACT.Exp)

        ident = const.tile([P, P], F32)
        masks.make_identity(nc, ident[:])

        bias = const.tile([P, 8], F32)

        x_codes = keep.tile([P, N_BLOCKS * F_PASSES * P], U32, align_bytes=64)
        x_scales = keep.tile([P, N_BLOCKS * F_PASSES * P], U8, align_bytes=64)
        w_codes = keep.tile([P, 8 * F_PASSES * P], U32, align_bytes=64)
        w_scales = keep.tile([P, 8 * F_PASSES * P], U8, align_bytes=64)
        k_codes = keep.tile([P, E_PASSES * K_DICT], U32, align_bytes=64)
        k_scales = keep.tile([P, E_PASSES * K_DICT], U8, align_bytes=64)
        q_codes = keep.tile([P, E_PASSES * N_ROWS], U32, align_bytes=64)
        q_scales = keep.tile([P, E_PASSES * N_ROWS], U8, align_bytes=64)
        q_grouped = [
            keep.tile([P, N_ROWS * 4], BF16, name="q_grouped%d" % g, align_bytes=64)
            for g in range(E_PASSES)
        ]

        def quantise(grouped, codes, scales, first, width):
            nc.vector.quantize_mx(
                out=codes[:, first : first + width].bitcast(FP8X4),
                scales=scales[:, first : first + width],
                in_=grouped,
            )

        def mx_pass(acc, a_codes, a_scales, a_first, b_codes, b_scales, b_first, width, g, passes):
            nc.tensor.matmul_mx(
                out=acc,
                lhsT=a_codes[:, a_first : a_first + P].bitcast(FP8X4),
                lhsT_scale=a_scales[:, a_first : a_first + P],
                rhs=b_codes[:, b_first : b_first + width].bitcast(FP8X4),
                rhs_scale=b_scales[:, b_first : b_first + width],
                start=(g == 0),
                stop=(g == passes - 1),
            )

        q_psum = ctx.enter_context(tc.psum_pool(name="q_psum", bufs=2))

        def new_q_banks():
            return [q_psum.tile([P, 4, P], F32, name="q_bank%d" % b, tag="q_bank") for b in range(2)]

        def first_product(c, s, a, q_banks):
            t = 2 * (c % 2) + s
            for b in range(2):
                for g in range(F_PASSES):
                    mx_pass(
                        q_banks[b][:, t, :],
                        w_codes, w_scales, ((2 * c + s) * F_PASSES + g) * P,
                        x_codes, x_scales, ((2 * a + b) * F_PASSES + g) * P,
                        P, g, F_PASSES,
                    )

        def finish_q(g, a, q_banks):
            bias_tn = bias[:, 4 * g : 4 * g + 4].unsqueeze(1).to_broadcast([P, P, 4])
            for b in range(2):
                i = 2 * a + b
                nc.vector.tensor_tensor(
                    out=q_grouped[g][:, BANK * i : BANK * (i + 1)].rearrange("p (n t) -> p n t", t=4),
                    in0=q_banks[b][:].rearrange("p t n -> p n t"),
                    in1=bias_tn,
                    op=ALU.add,
                )
            for b in range(2):
                i = 2 * a + b
                quantise(
                    q_grouped[g][:, BANK * i : BANK * (i + 1)], q_codes, q_scales, g * N_ROWS + P * i, P
                )

        x_units = [
            (x_raw[a], False, x_codes, x_scales, [2 * a * BANK, (2 * a + 1) * BANK]) for a in range(2)
        ]
        w_units = [
            (w_raw[c], False, w_codes, w_scales, [2 * c * BANK, (2 * c + 1) * BANK]) for c in range(4)
        ]
        k_units = [
            (k_raw[c], True, k_codes, k_scales, [BANK * c, K_DICT + BANK * c]) for c in range(J_CHUNKS)
        ]

        def quantise_unit(unit, grouped):
            for h in range(2):
                quantise(grouped[:, 2048 * h : 2048 * (h + 1)], unit[2], unit[3], unit[4][h], BANK)

        with tc.psum_pool(name="t_psum", bufs=6) as t_psum:

            def transpose_unit(unit):
                words = unit[0][:].bitcast(F32)
                grouped = grouped_pool.tile([P, UNIT], BF16, align_bytes=64)
                order = "p (g b r u) -> p b g r u" if unit[1] else "p (b g r u) -> p b g r u"
                dest = grouped[:].bitcast(F32).rearrange(order, g=2, b=4, u=2)
                for b in range(4):
                    bank = t_psum.tile([P, 4, P], F32)
                    for v in range(4):
                        first = BANK * b + P * v
                        nc.tensor.transpose(bank[:, v, :], words[:, first : first + P], ident[:])
                    planes = bank[:].rearrange("p (g u) r -> p g r u", u=2)
                    if b == 0:
                        nc.vector.tensor_copy(out=dest[:, b], in_=planes)
                    else:
                        nc.scalar.copy(out=dest[:, b], in_=planes)
                return grouped

            for unit in [x_units[0], w_units[0]]:
                quantise_unit(unit, transpose_unit(unit))
            later_units = w_units[1:] + k_units
            q_banks = []
            for group in range(8):
                c, s = divmod(group, 2)
                grouped = transpose_unit(later_units[group]) if group < len(later_units) else None
                if group % 4 == 0:
                    q_banks = new_q_banks()
                first_product(c, s, 0, q_banks)
                if group == 0:
                    nc.vector.tensor_copy(out=bias[:], in_=bias_bf[:])
                if group % 4 == 3:
                    finish_q(group // 4, 0, q_banks)
                if group < len(later_units):
                    quantise_unit(later_units[group], grouped)
            quantise_unit(x_units[1], transpose_unit(x_units[1]))

        with tc.psum_pool(name="s_psum", bufs=6, reuse_waits="tile") as s_psum:

            def scores(i):
                banks = []
                for c in range(J_CHUNKS):
                    bank = s_psum.tile([P, BANK], F32, name="s_bank")
                    for g in range(E_PASSES):
                        mx_pass(
                            bank[:],
                            q_codes, q_scales, g * N_ROWS + P * i,
                            k_codes, k_scales, g * K_DICT + BANK * c,
                            BANK, g, E_PASSES,
                        )
                    banks.append(bank)
                return banks

            def row_maximum(banks):
                chunk_max = small.tile([P, J_CHUNKS], F32)
                for c in range(J_CHUNKS):
                    nc.vector.tensor_reduce(
                        out=chunk_max[:, c : c + 1], in_=banks[c][:], axis=AXIS.X, op=ALU.max
                    )
                row_max = small.tile([P, 1], F32)
                nc.vector.tensor_reduce(out=row_max[:], in_=chunk_max[:], axis=AXIS.X, op=ALU.max)
                shift = small.tile([P, 1], F32)
                nc.vector.tensor_scalar_mul(shift[:], row_max[:], -SCALE)
                return shift

            def maximum_of(i):
                banks = scores(i)
                return banks, row_maximum(banks)

            def exponentials(banks, shift):
                e = soft.tile([P, K_DICT], F32)
                result = soft.tile([P, K_DICT], F32)
                chunk_sum = small.tile([P, J_CHUNKS], F32)
                for c in range(J_CHUNKS):
                    cols = slice(BANK * c, BANK * (c + 1))
                    nc.scalar.activation(
                        out=e[:, cols],
                        in_=banks[c][:],
                        func=ACT.Exp,
                        bias=shift[:],
                        scale=SCALE,
                        accum_out=chunk_sum[:, c : c + 1],
                    )
                    if c < J_CHUNKS - 1:
                        nc.gpsimd.tensor_tensor(
                            out=result[:, cols], in0=e[:, cols], in1=prior_all[:, cols], op=ALU.mult
                        )
                return e, result, chunk_sum

            def normalise_and_store(i, e, result, chunk_sum):
                rows = out[P * i : P * (i + 1), :]
                first, last = slice(0, K_DICT - BANK), slice(K_DICT - BANK, K_DICT)
                row_sum = small.tile([P, 1], F32)
                nc.vector.tensor_reduce(out=row_sum[:], in_=chunk_sum[:], axis=AXIS.X, op=ALU.add)
                inverse = small.tile([P, 1], F32)
                nc.vector.reciprocal(inverse[:], row_sum[:])
                nc.vector.scalar_tensor_tensor(
                    out=result[:, last],
                    in0=e[:, last],
                    scalar=inverse[:],
                    in1=prior_all[:, last],
                    op0=ALU.mult,
                    op1=ALU.mult,
                )
                nc.sync.dma_start(out=rows[:, last], in_=result[:, last])
                nc.scalar.activation(
                    out=result[:, first], in_=result[:, first], func=ACT.Copy, scale=inverse[:]
                )
                nc.sync.dma_start(out=rows[:, first], in_=result[:, first])

            started = [exponentials(*maximum_of(i)) for i in range(2)]
            q_banks = new_q_banks()
            for t in range(4):
                first_product(t // 2, t % 2, 1, q_banks)
            finish_q(0, 1, q_banks)
            normalise_and_store(0, *started[0])
            q_banks = new_q_banks()
            for t in range(4):
                first_product(2 + t // 2, t % 2, 1, q_banks)
            normalise_and_store(1, *started[1])
            finish_q(1, 1, q_banks)
            started = [exponentials(*maximum_of(i)) for i in range(2, 4)]
            normalise_and_store(2, *started[0])
            normalise_and_store(3, *started[1])
